import numpy as np
import ml_dtypes

BF16 = ml_dtypes.bfloat16


def bf(x):
    return np.asarray(x, np.float32).astype(BF16)


def f32(x):
    return np.asarray(x, np.float32)


def f64(x):
    return np.asarray(x).astype(np.float64)


def striped(idx):
    return np.tile(idx.reshape(-1, 16).T, (8, 1))


C, K, M, S, N = 256, 512, 1024, 4096, 1024


def sigmoid(v):
    return 1.0 / (1.0 + np.exp(-v))


def xavier(fan_in, fan_out):
    lim = np.sqrt(6.0 / (fan_in + fan_out))
    return np.random.uniform(-lim, lim, (fan_in, fan_out))


def setup_inputs():
    return {"base": f32(0.5 * np.random.standard_normal((C, S))), "x": bf(np.random.standard_normal((K, N))), "w_ih": bf(xavier(K, M)), "h0": bf(np.random.standard_normal((C, N))), "w_hh": bf(xavier(C, M)), "b": f32(0.1 * np.random.standard_normal((M, 1))), "c0": f32(np.random.standard_normal((C, N))), "offs": striped(np.random.permutation(S)[:N])}


def reference(base, x, w_ih, h0, w_hh, b, c0, offs):
    idx = offs[:16].T.reshape(-1)
    z = f64(w_ih).T @ f64(x) + f64(w_hh).T @ f64(h0) + f64(b)
    zi, zf, zu, zo = z.reshape(-1, C, N)
    c1 = sigmoid(zf) * f64(c0) + sigmoid(zi) * np.tanh(zu)
    out = f64(base).copy()
    out[:, idx] = sigmoid(zo) * np.tanh(c1)
    return out

@@ -1,0 +1,93 @@
+import concourse.mybir as mybir
+
+F32, BF16, U16 = mybir.dt.float32, mybir.dt.bfloat16, mybir.dt.uint16
+SIGMOID = mybir.ActivationFunctionType.Sigmoid
+TANH = mybir.ActivationFunctionType.Tanh
+MULT = mybir.AluOpType.mult
+
+P = 128
+CHANNELS, SLOTS, SAMPLES = 256, 4096, 1024
+IN_ROWS, HIDDEN_ROWS = 512, 256
+BANK = 512
+CHANNEL_BLOCKS = CHANNELS // P
+SAMPLE_PIECES = SAMPLES // BANK
+
+GATES = {
+    "i": (0 * CHANNELS, SIGMOID),
+    "f": (1 * CHANNELS, SIGMOID),
+    "u": (2 * CHANNELS, TANH),
+    "o": (3 * CHANNELS, SIGMOID),
+}
+
+FLOPS = 2 * (IN_ROWS + HIDDEN_ROWS) * 4 * CHANNELS * SAMPLES
+
+
+def tile_decodercell_kernel(tc, base, x, w_ih, h0, w_hh, b, c0, offs, out):
+    nc = tc.nc
+    with (
+        tc.tile_pool(name="held", bufs=1) as held,
+        tc.tile_pool(name="work", bufs=CHANNEL_BLOCKS) as work,
+        tc.psum_pool(name="psum", bufs=8) as psum,
+    ):
+        offsets = held.tile([P, SAMPLES // 16], U16, name="offsets")
+        nc.sync.dma_start(offsets[:], offs)
+
+        row_blocks = [(w_ih, x, r) for r in range(IN_ROWS // P)]
+        row_blocks += [(w_hh, h0, r) for r in range(HIDDEN_ROWS // P)]
+        weights, moving = [], []
+        for k, (w_dram, in_dram, r) in enumerate(row_blocks):
+            w_k = held.tile([P, 4 * CHANNELS], BF16, name=f"w{k}")
+            in_k = held.tile([P, SAMPLES], BF16, name=f"in{k}")
+            nc.sync.dma_start(w_k[:], w_dram[r * P : (r + 1) * P, :])
+            nc.sync.dma_start(in_k[:], in_dram[r * P : (r + 1) * P, :])
+            weights.append(w_k)
+            moving.append(in_k)
+
+        bias = held.tile([P, 4 * CHANNEL_BLOCKS], F32, name="bias")
+        with nc.allow_non_contiguous_dma(reason="1,024 floats, one to a partition and column"):
+            nc.gpsimd.dma_start(bias[:], b.rearrange("(m p) one -> p (m one)", p=P))
+
+        old_cells, windows = [], []
+        for cb in range(CHANNEL_BLOCKS):
+            old_cell = held.tile([P, SAMPLES], F32, name=f"old_cell{cb}")
+            window = held.tile([P, SLOTS], F32, name=f"window{cb}")
+            nc.sync.dma_start(old_cell[:], c0[cb * P : (cb + 1) * P, :])
+            nc.sync.dma_start(window[:], base[cb * P : (cb + 1) * P, :])
+            old_cells.append(old_cell)
+            windows.append(window)
+
+        def gate(name, cb):
+            first_row, func = GATES[name]
+            row = first_row + cb * P
+            value = work.tile([P, SAMPLES], F32, name=f"gate_{name}")
+            for piece in range(SAMPLE_PIECES):
+                cols = slice(piece * BANK, (piece + 1) * BANK)
+                z = psum.tile([P, BANK], F32, name="z")
+                for k in range(len(row_blocks)):
+                    nc.tensor.matmul(
+                        z[:],
+                        weights[k][:, row : row + P],
+                        moving[k][:, cols],
+                        start=(k == 0),
+                        stop=(k == len(row_blocks) - 1),
+                    )
+                nc.scalar.activation(value[:, cols], z[:], func, bias=bias[:, row // P : row // P + 1])
+            return value
+
+        for cb in range(CHANNEL_BLOCKS):
+            gate_i = gate("i", cb)
+            gate_u = gate("u", cb)
+            gate_f = gate("f", cb)
+
+            fresh = work.tile([P, SAMPLES], F32, name="fresh")
+            cell = work.tile([P, SAMPLES], F32, name="cell")
+            tanh_cell = work.tile([P, SAMPLES], F32, name="tanh_cell")
+            nc.vector.tensor_mul(fresh[:], gate_i[:], gate_u[:])
+            nc.vector.tensor_mul(cell[:], gate_f[:], old_cells[cb][:])
+            nc.vector.tensor_add(cell[:], cell[:], fresh[:])
+            nc.scalar.activation(tanh_cell[:], cell[:], TANH)
+
+            gate_o = gate("o", cb)
+
+            nc.vector.tensor_tensor(windows[cb][:].indirect(offsets[:]), gate_o[:], tanh_cell[:], MULT)
+            nc.sync.dma_start(out[cb * P : (cb + 1) * P, :], windows[cb][:])

@@ -29,9 +29,6 @@ def tile_decodercell_kernel(tc, base, x, w_ih, h0, w_hh, b, c0, offs, out):
         tc.tile_pool(name="work", bufs=CHANNEL_BLOCKS) as work,
         tc.psum_pool(name="psum", bufs=8) as psum,
     ):
-        offsets = held.tile([P, SAMPLES // 16], U16, name="offsets")
-        nc.sync.dma_start(offsets[:], offs)
-
         row_blocks = [(w_ih, x, r) for r in range(IN_ROWS // P)]
         row_blocks += [(w_hh, h0, r) for r in range(HIDDEN_ROWS // P)]
         weights, moving = [], []
@@ -45,7 +42,10 @@ def tile_decodercell_kernel(tc, base, x, w_ih, h0, w_hh, b, c0, offs, out):
 
         bias = held.tile([P, 4 * CHANNEL_BLOCKS], F32, name="bias")
         with nc.allow_non_contiguous_dma(reason="1,024 floats, one to a partition and column"):
-            nc.gpsimd.dma_start(bias[:], b.rearrange("(m p) one -> p (m one)", p=P))
+            nc.scalar.dma_start(bias[:], b.rearrange("(m p) one -> p (m one)", p=P))
+
+        offsets = held.tile([P, SAMPLES // 16], U16, name="offsets")
+        nc.sync.dma_start(offsets[:], offs)
 
         old_cells, windows = [], []
         for cb in range(CHANNEL_BLOCKS):
@@ -82,10 +82,14 @@ def tile_decodercell_kernel(tc, base, x, w_ih, h0, w_hh, b, c0, offs, out):
             fresh = work.tile([P, SAMPLES], F32, name="fresh")
             cell = work.tile([P, SAMPLES], F32, name="cell")
             tanh_cell = work.tile([P, SAMPLES], F32, name="tanh_cell")
-            nc.vector.tensor_mul(fresh[:], gate_i[:], gate_u[:])
-            nc.vector.tensor_mul(cell[:], gate_f[:], old_cells[cb][:])
-            nc.vector.tensor_add(cell[:], cell[:], fresh[:])
-            nc.scalar.activation(tanh_cell[:], cell[:], TANH)
+            for piece in range(SAMPLE_PIECES):
+                cols = slice(piece * BANK, (piece + 1) * BANK)
+                nc.vector.tensor_mul(fresh[:, cols], gate_i[:, cols], gate_u[:, cols])
+            for piece in range(SAMPLE_PIECES):
+                cols = slice(piece * BANK, (piece + 1) * BANK)
+                nc.vector.tensor_mul(cell[:, cols], gate_f[:, cols], old_cells[cb][:, cols])
+                nc.vector.tensor_add(cell[:, cols], cell[:, cols], fresh[:, cols])
+                nc.scalar.activation(tanh_cell[:, cols], cell[:, cols], TANH)
 
             gate_o = gate("o", cb)
 

@@ -11,6 +11,7 @@ IN_ROWS, HIDDEN_ROWS = 512, 256
 BANK = 512
 CHANNEL_BLOCKS = CHANNELS // P
 SAMPLE_PIECES = SAMPLES // BANK
+WARM_UP_MATMULS = 8
 
 GATES = {
     "i": (0 * CHANNELS, SIGMOID),
@@ -29,6 +30,12 @@ def tile_decodercell_kernel(tc, base, x, w_ih, h0, w_hh, b, c0, offs, out):
         tc.tile_pool(name="work", bufs=CHANNEL_BLOCKS) as work,
         tc.psum_pool(name="psum", bufs=8) as psum,
     ):
+        zeros = held.tile([P, BANK], BF16, name="zeros")
+        nc.vector.memset(zeros[:], 0.0)
+        z = psum.tile([P, BANK], F32, name="z")
+        for repeat in range(WARM_UP_MATMULS):
+            nc.tensor.matmul(z[:], zeros[:, 0:P], zeros[:], start=True, stop=True)
+
         row_blocks = [(w_ih, x, r) for r in range(IN_ROWS // P)]
         row_blocks += [(w_hh, h0, r) for r in range(HIDDEN_ROWS // P)]
         weights, moving = [], []
@@ -42,7 +49,7 @@ def tile_decodercell_kernel(tc, base, x, w_ih, h0, w_hh, b, c0, offs, out):
 
         bias = held.tile([P, 4 * CHANNEL_BLOCKS], F32, name="bias")
         with nc.allow_non_contiguous_dma(reason="1,024 floats, one to a partition and column"):
-            nc.scalar.dma_start(bias[:], b.rearrange("(m p) one -> p (m one)", p=P))
+            nc.sync.dma_start(bias[:], b.rearrange("(m p) one -> p (m one)", p=P))
 
         offsets = held.tile([P, SAMPLES // 16], U16, name="offsets")
         nc.sync.dma_start(offsets[:], offs)

@@ -31,7 +31,7 @@ def tile_decodercell_kernel(tc, base, x, w_ih, h0, w_hh, b, c0, offs, out):
         tc.psum_pool(name="psum", bufs=8) as psum,
     ):
         zeros = held.tile([P, BANK], BF16, name="zeros")
-        nc.vector.memset(zeros[:], 0.0)
+        nc.gpsimd.memset(zeros[:], 0.0)
         z = psum.tile([P, BANK], F32, name="z")
         for repeat in range(WARM_UP_MATMULS):
             nc.tensor.matmul(z[:], zeros[:, 0:P], zeros[:], start=True, stop=True)
@@ -49,7 +49,7 @@ def tile_decodercell_kernel(tc, base, x, w_ih, h0, w_hh, b, c0, offs, out):
 
         bias = held.tile([P, 4 * CHANNEL_BLOCKS], F32, name="bias")
         with nc.allow_non_contiguous_dma(reason="1,024 floats, one to a partition and column"):
-            nc.sync.dma_start(bias[:], b.rearrange("(m p) one -> p (m one)", p=P))
+            nc.gpsimd.dma_start(bias[:], b.rearrange("(m p) one -> p (m one)", p=P))
 
         offsets = held.tile([P, SAMPLES // 16], U16, name="offsets")
         nc.sync.dma_start(offsets[:], offs)

@@ -8,10 +8,11 @@ MULT = mybir.AluOpType.mult
 P = 128
 CHANNELS, SLOTS, SAMPLES = 256, 4096, 1024
 IN_ROWS, HIDDEN_ROWS = 512, 256
-BANK = 512
+Z_ROWS = 4 * CHANNELS
 CHANNEL_BLOCKS = CHANNELS // P
-SAMPLE_PIECES = SAMPLES // BANK
-WARM_UP_MATMULS = 8
+PSUM_BANKS = 8
+PIECE = 512
+PIECES = SAMPLES // PIECE
 
 GATES = {
     "i": (0 * CHANNELS, SIGMOID),
@@ -20,7 +21,9 @@ GATES = {
     "o": (3 * CHANNELS, SIGMOID),
 }
 
-FLOPS = 2 * (IN_ROWS + HIDDEN_ROWS) * 4 * CHANNELS * SAMPLES
+WARM_UP_MATMULS = 8
+
+FLOPS = 2 * (IN_ROWS + HIDDEN_ROWS) * Z_ROWS * SAMPLES
 
 
 def tile_decodercell_kernel(tc, base, x, w_ih, h0, w_hh, b, c0, offs, out):
@@ -28,28 +31,28 @@ def tile_decodercell_kernel(tc, base, x, w_ih, h0, w_hh, b, c0, offs, out):
     with (
         tc.tile_pool(name="held", bufs=1) as held,
         tc.tile_pool(name="work", bufs=CHANNEL_BLOCKS) as work,
-        tc.psum_pool(name="psum", bufs=8) as psum,
+        tc.psum_pool(name="psum", bufs=PSUM_BANKS) as psum,
     ):
-        zeros = held.tile([P, BANK], BF16, name="zeros")
-        nc.gpsimd.memset(zeros[:], 0.0)
-        z = psum.tile([P, BANK], F32, name="z")
+        zeros = held.tile([P, PIECE], BF16, name="zeros")
+        nc.vector.memset(zeros[:], 0.0)
+        warm_up_product = psum.tile([P, PIECE], F32, name="warm_up_product", tag="z")
         for repeat in range(WARM_UP_MATMULS):
-            nc.tensor.matmul(z[:], zeros[:, 0:P], zeros[:], start=True, stop=True)
+            nc.tensor.matmul(warm_up_product[:], zeros[:, 0:P], zeros[:], start=True, stop=True)
 
         row_blocks = [(w_ih, x, r) for r in range(IN_ROWS // P)]
         row_blocks += [(w_hh, h0, r) for r in range(HIDDEN_ROWS // P)]
         weights, moving = [], []
         for k, (w_dram, in_dram, r) in enumerate(row_blocks):
-            w_k = held.tile([P, 4 * CHANNELS], BF16, name=f"w{k}")
+            w_k = held.tile([P, Z_ROWS], BF16, name=f"w{k}")
             in_k = held.tile([P, SAMPLES], BF16, name=f"in{k}")
             nc.sync.dma_start(w_k[:], w_dram[r * P : (r + 1) * P, :])
             nc.sync.dma_start(in_k[:], in_dram[r * P : (r + 1) * P, :])
             weights.append(w_k)
             moving.append(in_k)
 
-        bias = held.tile([P, 4 * CHANNEL_BLOCKS], F32, name="bias")
-        with nc.allow_non_contiguous_dma(reason="1,024 floats, one to a partition and column"):
-            nc.gpsimd.dma_start(bias[:], b.rearrange("(m p) one -> p (m one)", p=P))
+        bias = held.tile([P, Z_ROWS // P], F32, name="bias")
+        with nc.allow_non_contiguous_dma(reason="1,024 floats, each to its own partition and column"):
+            nc.sync.dma_start(bias[:], b.rearrange("(m p) one -> p (m one)", p=P))
 
         offsets = held.tile([P, SAMPLES // 16], U16, name="offsets")
         nc.sync.dma_start(offsets[:], offs)
@@ -66,10 +69,11 @@ def tile_decodercell_kernel(tc, base, x, w_ih, h0, w_hh, b, c0, offs, out):
         def gate(name, cb):
             first_row, func = GATES[name]
             row = first_row + cb * P
+            bias_column = bias[:, row // P : row // P + 1]
             value = work.tile([P, SAMPLES], F32, name=f"gate_{name}")
-            for piece in range(SAMPLE_PIECES):
-                cols = slice(piece * BANK, (piece + 1) * BANK)
-                z = psum.tile([P, BANK], F32, name="z")
+            for piece in range(PIECES):
+                cols = slice(piece * PIECE, (piece + 1) * PIECE)
+                z = psum.tile([P, PIECE], F32, name="z")
                 for k in range(len(row_blocks)):
                     nc.tensor.matmul(
                         z[:],
@@ -78,7 +82,7 @@ def tile_decodercell_kernel(tc, base, x, w_ih, h0, w_hh, b, c0, offs, out):
                         start=(k == 0),
                         stop=(k == len(row_blocks) - 1),
                     )
-                nc.scalar.activation(value[:, cols], z[:], func, bias=bias[:, row // P : row // P + 1])
+                nc.scalar.activation(value[:, cols], z[:], func, bias=bias_column)
             return value
 
         for cb in range(CHANNEL_BLOCKS):
@@ -86,16 +90,17 @@ def tile_decodercell_kernel(tc, base, x, w_ih, h0, w_hh, b, c0, offs, out):
             gate_u = gate("u", cb)
             gate_f = gate("f", cb)
 
-            fresh = work.tile([P, SAMPLES], F32, name="fresh")
+            added = work.tile([P, SAMPLES], F32, name="added")
+            kept = work.tile([P, SAMPLES], F32, name="kept")
             cell = work.tile([P, SAMPLES], F32, name="cell")
             tanh_cell = work.tile([P, SAMPLES], F32, name="tanh_cell")
-            for piece in range(SAMPLE_PIECES):
-                cols = slice(piece * BANK, (piece + 1) * BANK)
-                nc.vector.tensor_mul(fresh[:, cols], gate_i[:, cols], gate_u[:, cols])
-            for piece in range(SAMPLE_PIECES):
-                cols = slice(piece * BANK, (piece + 1) * BANK)
-                nc.vector.tensor_mul(cell[:, cols], gate_f[:, cols], old_cells[cb][:, cols])
-                nc.vector.tensor_add(cell[:, cols], cell[:, cols], fresh[:, cols])
+            for piece in range(PIECES):
+                cols = slice(piece * PIECE, (piece + 1) * PIECE)
+                nc.vector.tensor_mul(added[:, cols], gate_i[:, cols], gate_u[:, cols])
+            for piece in range(PIECES):
+                cols = slice(piece * PIECE, (piece + 1) * PIECE)
+                nc.vector.tensor_mul(kept[:, cols], gate_f[:, cols], old_cells[cb][:, cols])
+                nc.vector.tensor_add(cell[:, cols], kept[:, cols], added[:, cols])
                 nc.scalar.activation(tanh_cell[:, cols], cell[:, cols], TANH)
 
             gate_o = gate("o", cb)

@@ -105,5 +105,8 @@ def tile_decodercell_kernel(tc, base, x, w_ih, h0, w_hh, b, c0, offs, out):
 
             gate_o = gate("o", cb)
 
-            nc.vector.tensor_tensor(windows[cb][:].indirect(offsets[:]), gate_o[:], tanh_cell[:], MULT)
+            for piece in range(PIECES):
+                cols = slice(piece * PIECE, (piece + 1) * PIECE)
+                listed = offsets[:, cols.start // 16 : cols.stop // 16]
+                nc.vector.tensor_tensor(windows[cb][:].indirect(listed), gate_o[:, cols], tanh_cell[:, cols], MULT)
             nc.sync.dma_start(out[cb * P : (cb + 1) * P, :], windows[cb][:])

@@ -21,7 +21,7 @@ GATES = {
     "o": (3 * CHANNELS, SIGMOID),
 }
 
-WARM_UP_MATMULS = 8
+WARM_UP_MATMULS = 4
 
 FLOPS = 2 * (IN_ROWS + HIDDEN_ROWS) * Z_ROWS * SAMPLES
 

@@ -23,6 +23,10 @@ GATES = {
 
 WARM_UP_MATMULS = 4
 
+assert Z_ROWS == SAMPLES
+WHOLE = slice(0, SAMPLES)
+FIRST_HALF, SECOND_HALF = slice(0, SAMPLES // 2), slice(SAMPLES // 2, SAMPLES)
+
 FLOPS = 2 * (IN_ROWS + HIDDEN_ROWS) * Z_ROWS * SAMPLES
 
 
@@ -45,8 +49,9 @@ def tile_decodercell_kernel(tc, base, x, w_ih, h0, w_hh, b, c0, offs, out):
         for k, (w_dram, in_dram, r) in enumerate(row_blocks):
             w_k = held.tile([P, Z_ROWS], BF16, name=f"w{k}")
             in_k = held.tile([P, SAMPLES], BF16, name=f"in{k}")
-            nc.sync.dma_start(w_k[:], w_dram[r * P : (r + 1) * P, :])
-            nc.sync.dma_start(in_k[:], in_dram[r * P : (r + 1) * P, :])
+            for cols in (FIRST_HALF, SECOND_HALF) if k == 0 else (WHOLE,):
+                nc.sync.dma_start(w_k[:, cols], w_dram[r * P : (r + 1) * P, cols])
+                nc.sync.dma_start(in_k[:, cols], in_dram[r * P : (r + 1) * P, cols])
             weights.append(w_k)
             moving.append(in_k)
 

@@ -10,7 +10,7 @@ CHANNELS, SLOTS, SAMPLES = 256, 4096, 1024
 IN_ROWS, HIDDEN_ROWS = 512, 256
 Z_ROWS = 4 * CHANNELS
 CHANNEL_BLOCKS = CHANNELS // P
-PSUM_BANKS = 8
+PSUM_BANKS = 6
 PIECE = 512
 PIECES = SAMPLES // PIECE
 
@@ -22,10 +22,6 @@ GATES = {
 }
 
 WARM_UP_MATMULS = 4
-
-assert Z_ROWS == SAMPLES
-WHOLE = slice(0, SAMPLES)
-FIRST_HALF, SECOND_HALF = slice(0, SAMPLES // 2), slice(SAMPLES // 2, SAMPLES)
 
 FLOPS = 2 * (IN_ROWS + HIDDEN_ROWS) * Z_ROWS * SAMPLES
 
@@ -43,17 +39,14 @@ def tile_decodercell_kernel(tc, base, x, w_ih, h0, w_hh, b, c0, offs, out):
         for repeat in range(WARM_UP_MATMULS):
             nc.tensor.matmul(warm_up_product[:], zeros[:, 0:P], zeros[:], start=True, stop=True)
 
-        row_blocks = [(w_ih, x, r) for r in range(IN_ROWS // P)]
-        row_blocks += [(w_hh, h0, r) for r in range(HIDDEN_ROWS // P)]
-        weights, moving = [], []
-        for k, (w_dram, in_dram, r) in enumerate(row_blocks):
-            w_k = held.tile([P, Z_ROWS], BF16, name=f"w{k}")
-            in_k = held.tile([P, SAMPLES], BF16, name=f"in{k}")
-            for cols in (FIRST_HALF, SECOND_HALF) if k == 0 else (WHOLE,):
-                nc.sync.dma_start(w_k[:, cols], w_dram[r * P : (r + 1) * P, cols])
-                nc.sync.dma_start(in_k[:, cols], in_dram[r * P : (r + 1) * P, cols])
-            weights.append(w_k)
-            moving.append(in_k)
+        row_blocks = []
+        for w_dram, in_dram, first, count in ((w_ih, x, 0, 1), (w_ih, x, 1, 1), (w_ih, x, 2, 2), (w_hh, h0, 0, 2)):
+            rows = slice(first * P, (first + count) * P)
+            w_group = held.tile([P, count, Z_ROWS], BF16, name=f"w{len(row_blocks)}")
+            in_group = held.tile([P, count, SAMPLES], BF16, name=f"in{len(row_blocks)}")
+            nc.sync.dma_start(w_group[:], w_dram[rows, :].rearrange("(r p) c -> p r c", p=P))
+            nc.sync.dma_start(in_group[:], in_dram[rows, :].rearrange("(r p) c -> p r c", p=P))
+            row_blocks += [(w_group[:, r, :], in_group[:, r, :]) for r in range(count)]
 
         bias = held.tile([P, Z_ROWS // P], F32, name="bias")
         with nc.allow_non_contiguous_dma(reason="1,024 floats, each to its own partition and column"):
@@ -79,11 +72,11 @@ def tile_decodercell_kernel(tc, base, x, w_ih, h0, w_hh, b, c0, offs, out):
             for piece in range(PIECES):
                 cols = slice(piece * PIECE, (piece + 1) * PIECE)
                 z = psum.tile([P, PIECE], F32, name="z")
-                for k in range(len(row_blocks)):
+                for k, (weights, moving) in enumerate(row_blocks):
                     nc.tensor.matmul(
                         z[:],
-                        weights[k][:, row : row + P],
-                        moving[k][:, cols],
+                        weights[:, row : row + P],
+                        moving[:, cols],
                         start=(k == 0),
                         stop=(k == len(row_blocks) - 1),
                     )
@@ -105,6 +98,8 @@ def tile_decodercell_kernel(tc, base, x, w_ih, h0, w_hh, b, c0, offs, out):
             for piece in range(PIECES):
                 cols = slice(piece * PIECE, (piece + 1) * PIECE)
                 nc.vector.tensor_mul(kept[:, cols], gate_f[:, cols], old_cells[cb][:, cols])
+            for piece in range(PIECES):
+                cols = slice(piece * PIECE, (piece + 1) * PIECE)
                 nc.vector.tensor_add(cell[:, cols], kept[:, cols], added[:, cols])
                 nc.scalar.activation(tanh_cell[:, cols], cell[:, cols], TANH)
 

@@ -13,6 +13,9 @@ CHANNEL_BLOCKS = CHANNELS // P
 PSUM_BANKS = 6
 PIECE = 512
 PIECES = SAMPLES // PIECE
+FIRST_PIECE, SECOND_PIECE = slice(0, PIECE), slice(PIECE, SAMPLES)
+PIECES_OF_SAMPLES = (FIRST_PIECE, SECOND_PIECE)
+HALVES_OF_FIRST_PIECE = (slice(0, PIECE // 2), slice(PIECE // 2, PIECE))
 
 GATES = {
     "i": (0 * CHANNELS, SIGMOID),
@@ -64,23 +67,23 @@ def tile_decodercell_kernel(tc, base, x, w_ih, h0, w_hh, b, c0, offs, out):
             old_cells.append(old_cell)
             windows.append(window)
 
-        def gate(name, cb):
+        def gate(name, cb, column_groups=PIECES_OF_SAMPLES):
             first_row, func = GATES[name]
             row = first_row + cb * P
             bias_column = bias[:, row // P : row // P + 1]
             value = work.tile([P, SAMPLES], F32, name=f"gate_{name}")
-            for piece in range(PIECES):
-                cols = slice(piece * PIECE, (piece + 1) * PIECE)
+            for cols in column_groups:
+                width = cols.stop - cols.start
                 z = psum.tile([P, PIECE], F32, name="z")
                 for k, (weights, moving) in enumerate(row_blocks):
                     nc.tensor.matmul(
-                        z[:],
+                        z[:, 0:width],
                         weights[:, row : row + P],
                         moving[:, cols],
                         start=(k == 0),
                         stop=(k == len(row_blocks) - 1),
                     )
-                nc.scalar.activation(value[:, cols], z[:], func, bias=bias_column)
+                nc.scalar.activation(value[:, cols], z[:, 0:width], func, bias=bias_column)
             return value
 
         for cb in range(CHANNEL_BLOCKS):
@@ -103,7 +106,8 @@ def tile_decodercell_kernel(tc, base, x, w_ih, h0, w_hh, b, c0, offs, out):
                 nc.vector.tensor_add(cell[:, cols], kept[:, cols], added[:, cols])
                 nc.scalar.activation(tanh_cell[:, cols], cell[:, cols], TANH)
 
-            gate_o = gate("o", cb)
+            last = cb == CHANNEL_BLOCKS - 1
+            gate_o = gate("o", cb, (*HALVES_OF_FIRST_PIECE, SECOND_PIECE) if last else PIECES_OF_SAMPLES)
 
             for piece in range(PIECES):
                 cols = slice(piece * PIECE, (piece + 1) * PIECE)

import concourse.mybir as mybir

F32, BF16, U16 = mybir.dt.float32, mybir.dt.bfloat16, mybir.dt.uint16
SIGMOID = mybir.ActivationFunctionType.Sigmoid
TANH = mybir.ActivationFunctionType.Tanh
MULT = mybir.AluOpType.mult

P = 128
CHANNELS, SLOTS, SAMPLES = 256, 4096, 1024
IN_ROWS, HIDDEN_ROWS = 512, 256
Z_ROWS = 4 * CHANNELS
CHANNEL_BLOCKS = CHANNELS // P
PSUM_BANKS = 6
PIECE = 512
PIECES = SAMPLES // PIECE
FIRST_PIECE, SECOND_PIECE = slice(0, PIECE), slice(PIECE, SAMPLES)
PIECES_OF_SAMPLES = (FIRST_PIECE, SECOND_PIECE)
HALVES_OF_FIRST_PIECE = (slice(0, PIECE // 2), slice(PIECE // 2, PIECE))

GATES = {
    "i": (0 * CHANNELS, SIGMOID),
    "f": (1 * CHANNELS, SIGMOID),
    "u": (2 * CHANNELS, TANH),
    "o": (3 * CHANNELS, SIGMOID),
}

WARM_UP_MATMULS = 4

FLOPS = 2 * (IN_ROWS + HIDDEN_ROWS) * Z_ROWS * SAMPLES


def tile_decodercell_kernel(tc, base, x, w_ih, h0, w_hh, b, c0, offs, out):
    nc = tc.nc
    with (
        tc.tile_pool(name="held", bufs=1) as held,
        tc.tile_pool(name="work", bufs=CHANNEL_BLOCKS) as work,
        tc.psum_pool(name="psum", bufs=PSUM_BANKS) as psum,
    ):
        zeros = held.tile([P, PIECE], BF16, name="zeros")
        nc.vector.memset(zeros[:], 0.0)
        warm_up_product = psum.tile([P, PIECE], F32, name="warm_up_product", tag="z")
        for repeat in range(WARM_UP_MATMULS):
            nc.tensor.matmul(warm_up_product[:], zeros[:, 0:P], zeros[:], start=True, stop=True)

        row_blocks = []
        for w_dram, in_dram, first, count in ((w_ih, x, 0, 1), (w_ih, x, 1, 1), (w_ih, x, 2, 2), (w_hh, h0, 0, 2)):
            rows = slice(first * P, (first + count) * P)
            w_group = held.tile([P, count, Z_ROWS], BF16, name=f"w{len(row_blocks)}")
            in_group = held.tile([P, count, SAMPLES], BF16, name=f"in{len(row_blocks)}")
            nc.sync.dma_start(w_group[:], w_dram[rows, :].rearrange("(r p) c -> p r c", p=P))
            nc.sync.dma_start(in_group[:], in_dram[rows, :].rearrange("(r p) c -> p r c", p=P))
            row_blocks += [(w_group[:, r, :], in_group[:, r, :]) for r in range(count)]

        bias = held.tile([P, Z_ROWS // P], F32, name="bias")
        with nc.allow_non_contiguous_dma(reason="1,024 floats, each to its own partition and column"):
            nc.sync.dma_start(bias[:], b.rearrange("(m p) one -> p (m one)", p=P))

        offsets = held.tile([P, SAMPLES // 16], U16, name="offsets")
        nc.sync.dma_start(offsets[:], offs)

        old_cells, windows = [], []
        for cb in range(CHANNEL_BLOCKS):
            old_cell = held.tile([P, SAMPLES], F32, name=f"old_cell{cb}")
            window = held.tile([P, SLOTS], F32, name=f"window{cb}")
            nc.sync.dma_start(old_cell[:], c0[cb * P : (cb + 1) * P, :])
            nc.sync.dma_start(window[:], base[cb * P : (cb + 1) * P, :])
            old_cells.append(old_cell)
            windows.append(window)

        def gate(name, cb, column_groups=PIECES_OF_SAMPLES):
            first_row, func = GATES[name]
            row = first_row + cb * P
            bias_column = bias[:, row // P : row // P + 1]
            value = work.tile([P, SAMPLES], F32, name=f"gate_{name}")
            for cols in column_groups:
                width = cols.stop - cols.start
                z = psum.tile([P, PIECE], F32, name="z")
                for k, (weights, moving) in enumerate(row_blocks):
                    nc.tensor.matmul(
                        z[:, 0:width],
                        weights[:, row : row + P],
                        moving[:, cols],
                        start=(k == 0),
                        stop=(k == len(row_blocks) - 1),
                    )
                nc.scalar.activation(value[:, cols], z[:, 0:width], func, bias=bias_column)
            return value

        for cb in range(CHANNEL_BLOCKS):
            gate_i = gate("i", cb)
            gate_u = gate("u", cb)
            gate_f = gate("f", cb)

            added = work.tile([P, SAMPLES], F32, name="added")
            kept = work.tile([P, SAMPLES], F32, name="kept")
            cell = work.tile([P, SAMPLES], F32, name="cell")
            tanh_cell = work.tile([P, SAMPLES], F32, name="tanh_cell")
            for piece in range(PIECES):
                cols = slice(piece * PIECE, (piece + 1) * PIECE)
                nc.vector.tensor_mul(added[:, cols], gate_i[:, cols], gate_u[:, cols])
            for piece in range(PIECES):
                cols = slice(piece * PIECE, (piece + 1) * PIECE)
                nc.vector.tensor_mul(kept[:, cols], gate_f[:, cols], old_cells[cb][:, cols])
            for piece in range(PIECES):
                cols = slice(piece * PIECE, (piece + 1) * PIECE)
                nc.vector.tensor_add(cell[:, cols], kept[:, cols], added[:, cols])
                nc.scalar.activation(tanh_cell[:, cols], cell[:, cols], TANH)

            last = cb == CHANNEL_BLOCKS - 1
            gate_o = gate("o", cb, (*HALVES_OF_FIRST_PIECE, SECOND_PIECE) if last else PIECES_OF_SAMPLES)

            for piece in range(PIECES):
                cols = slice(piece * PIECE, (piece + 1) * PIECE)
                listed = offsets[:, cols.start // 16 : cols.stop // 16]
                nc.vector.tensor_tensor(windows[cb][:].indirect(listed), gate_o[:, cols], tanh_cell[:, cols], MULT)
            nc.sync.dma_start(out[cb * P : (cb + 1) * P, :], windows[cb][:])
